import numpy as np
import ml_dtypes


def mxq(x, axis, fmt="e4m3"):
    dtype, down = {"e4m3": (ml_dtypes.float8_e4m3fn, 7), "e5m2": (ml_dtypes.float8_e5m2, 14)}[fmt]
    v = np.moveaxis(np.asarray(x, np.float32).astype(ml_dtypes.bfloat16).astype(np.float64), axis, -1)
    blocks = v.reshape(v.shape[:-1] + (-1, 32))
    amax = np.abs(blocks).max(-1, keepdims=True)
    byte = np.maximum(np.where(amax > 0, np.frexp(amax)[1] - 1 + 127, 0) - down, 1)
    scale = np.exp2(byte - 127.0)
    codes = (blocks / scale).astype(np.float32).astype(dtype).astype(np.float64)
    return np.moveaxis((codes * scale).reshape(v.shape), -1, axis)


WIDE = False


def mx_kscale(k):
    if not WIDE:
        return np.ones(k)
    levels = np.array([10, -10, 5, -5, 0])
    a = np.random.permutation(np.resize(levels, k // 512 * 4)).reshape(k // 512, 4)
    idx = np.arange(k)
    return np.exp2(a[idx // 512, idx % 128 // 32])


BF16 = ml_dtypes.bfloat16


def bf(x):
    return np.asarray(x, np.float32).astype(BF16)


def f64(x):
    return np.asarray(x).astype(np.float64)


B, T, N, H, G, GH = 32, 4, 8, 512, 9, 3


def sigmoid(v):
    return 1.0 / (1.0 + np.exp(-v))


def setup_inputs():
    s = mx_kscale(H)
    return {"h_new": bf(np.random.standard_normal((B, T, N, H)) * 0.35 * s),
            "c_new": bf(np.random.standard_normal((B, T, N, H)) * 0.8),
            "g_t": bf(np.random.standard_normal((B, N, H)) * s),
            "c_g_t": bf(np.random.standard_normal((B, N, H)) * 0.5),
            "Wg_t": bf(np.random.standard_normal((GH, T, H, H)) * 2.0 / np.sqrt(H) / s[:, None]),
            "Zg_t": bf(np.random.standard_normal((GH, T, H, H)) * 1.0 / np.sqrt(H) / s[:, None]),
            "bg_t": bf(np.random.standard_normal((GH, T, 1, H)) * 0.3)}


def reference(h_new, c_new, g_t, c_g_t, Wg_t, Zg_t, bg_t):
    c_new, c_g_t = f64(c_new), f64(c_g_t)
    hq = mxq(f64(h_new).transpose(1, 0, 2, 3).reshape(T, B * N, H), 2, "e4m3")
    preg = (hq @ mxq(f64(Wg_t), 2, "e4m3")) + f64(bg_t)
    zt_part = mxq(f64(g_t).reshape(B * N, H), 1, "e4m3") @ mxq(f64(Zg_t), 2, "e4m3")
    gates = sigmoid(preg + zt_part).reshape(GH, T, B, N, H).transpose(0, 2, 1, 3, 4)
    f_t, gg_t, o_t = gates
    c_g_t_new = np.mean(f_t * c_new, axis=1) + np.mean(gg_t, axis=1) * c_g_t
    g_t_new = np.mean(o_t, axis=1) * np.tanh(c_g_t_new)
    return g_t_new, c_g_t_new

@@ -1,0 +1,318 @@
+from contextlib import ExitStack
+
+import concourse.mybir as mybir
+from concourse.masks import make_identity
+
+BF16 = mybir.dt.bfloat16
+F32 = mybir.dt.float32
+U32 = mybir.dt.uint32
+U8 = mybir.dt.uint8
+FP8X4 = mybir.dt.float8_e4m3fn_x4
+ACT = mybir.ActivationFunctionType
+ALU = mybir.AluOpType
+
+P = 128
+PACK = 4
+SEQS, FRAMES, BONES, FEATS = 32, 4, 8, 512
+GATES = 3
+ROWS = SEQS * BONES
+ROW_TILES = ROWS // P
+FEAT_TILES = FEATS // P
+SLICES = SEQS * FRAMES * BONES // P
+SEQS_PER_SLICE = SEQS // SLICES
+COLS_PER_SLICE = SEQS_PER_SLICE * BONES
+STEPS = GATES * FRAMES
+RUN = 4
+RAW_BUFS = 10
+VECTOR_COLS_PLAIN = 352
+VECTOR_COLS_BUSY = 272
+FIRST_PRODUCT = FRAMES + 1
+COMBINE = 2 * FRAMES + 2
+
+FLOPS = 2 * 2 * GATES * FRAMES * ROWS * FEATS * FEATS
+
+
+def tile_st_hmr_pb_kernel(tc, h_new, c_new, g_t, c_g_t, Wg_t, Zg_t, bg_t, out_0, out_1):
+    nc = tc.nc
+    with ExitStack() as ctx:
+        keep = ctx.enter_context(tc.tile_pool(name="keep", bufs=1))
+        raw_pool = ctx.enter_context(tc.tile_pool(name="raw", bufs=RAW_BUFS))
+        grouped_pool = ctx.enter_context(tc.tile_pool(name="grouped", bufs=3))
+        code_pool = ctx.enter_context(tc.tile_pool(name="code", bufs=3))
+        gate_pool = ctx.enter_context(tc.tile_pool(name="gate", bufs=3))
+        prod_pool = ctx.enter_context(tc.tile_pool(name="prod", bufs=2))
+        psum_sum = ctx.enter_context(tc.psum_pool(name="psum_sum", bufs=2))
+        psum_acc = ctx.enter_context(tc.psum_pool(name="psum_acc", bufs=3))
+        psum_tr = ctx.enter_context(tc.psum_pool(name="psum_tr", bufs=1))
+
+        bias_rows = keep.tile([P, P], BF16)
+        nc.vector.memset(bias_rows[:], 0.0)
+        nc.scalar.dma_start(
+            out=bias_rows[0 : STEPS * FEAT_TILES, :],
+            in_=bg_t.rearrange("g t o (c f) -> (g t o c) f", f=P),
+        )
+
+        g_rows = keep.tile([P, ROW_TILES * FEATS], BF16)
+        nc.sync.dma_start(
+            out=g_rows[:].rearrange("p (b k) -> p b k", b=ROW_TILES),
+            in_=g_t.rearrange("r n k -> (r n) k").rearrange("(b p) k -> p b k", p=P),
+        )
+        h_rows = keep.tile([P, SLICES * FEATS], BF16)
+        h_rows_view = h_rows[:].rearrange("p (i k) -> p i k", i=SLICES)
+        h_dram = h_new.rearrange("r t n k -> (r t n) k").rearrange("(i p) k -> p i k", p=P)
+        for part in range(2):
+            some = slice(part * SLICES // 2, (part + 1) * SLICES // 2)
+            nc.sync.dma_start(out=h_rows_view[:, some, :], in_=h_dram[:, some, :])
+
+        raws = []
+
+        def load_weights(step):
+            gate, frame = divmod(step, FRAMES)
+            raw = raw_pool.tile([P, 2, PACK, FEATS], BF16, name="raw")
+            nc.sync.dma_start(out=raw[:, 0], in_=Wg_t[gate, frame].rearrange("(p j) n -> p j n", j=PACK))
+            nc.sync.dma_start(out=raw[:, 1], in_=Zg_t[gate, frame].rearrange("(p j) n -> p j n", j=PACK))
+            raws.append(raw)
+
+        c_rows = keep.tile([P, SLICES, FEATS], BF16)
+        cg_rows = keep.tile([P, ROW_TILES, FEATS], BF16)
+        for step in range(RAW_BUFS):
+            load_weights(step)
+            if step == FRAMES - 1:
+                nc.sync.dma_start(
+                    out=c_rows[:],
+                    in_=c_new.rearrange("r t n k -> (r t n) k").rearrange("(i p) k -> p i k", p=P),
+                )
+            if step == 2 * FRAMES - 1:
+                nc.sync.dma_start(
+                    out=cg_rows[:],
+                    in_=c_g_t.rearrange("r n k -> (r n) k").rearrange("(b p) k -> p b k", p=P),
+                )
+
+        warm = keep.tile([P, 1], F32)
+        nc.vector.memset(warm[:], 0.0)
+        nc.scalar.activation(out=warm[:], in_=warm[:], func=ACT.Sigmoid)
+
+        ident_f32 = keep.tile([P, P], F32)
+        make_identity(nc, ident_f32[:])
+        ident_bf16 = keep.tile([P, P], BF16)
+        nc.vector.tensor_copy(out=ident_bf16[:], in_=ident_f32[:])
+        perm_f32 = keep.tile([P, P], F32)
+        perm_bf16 = keep.tile([P, P], BF16)
+        by_frame = ident_f32[:].rearrange("p (a t n) -> p t a n", a=SEQS_PER_SLICE, t=FRAMES)
+        nc.vector.tensor_copy(
+            out=perm_f32[:].rearrange("p (t a n) -> p t a n", t=FRAMES, a=SEQS_PER_SLICE), in_=by_frame
+        )
+        nc.vector.tensor_copy(
+            out=perm_bf16[:].rearrange("p (t a n) -> p t a n", t=FRAMES, a=SEQS_PER_SLICE), in_=by_frame
+        )
+
+        bias_ps = psum_tr.tile([P, P], BF16, name="bias_ps", tag="tr")
+        nc.tensor.transpose(bias_ps[:], bias_rows[:], ident_bf16[:])
+        bias_cols = keep.tile([P, STEPS * FEAT_TILES], F32)
+        nc.vector.tensor_copy(out=bias_cols[:], in_=bias_ps[:, 0 : STEPS * FEAT_TILES])
+
+        g_grouped = keep.tile([P, ROWS * PACK], BF16, align_bytes=64)
+        g_codes = keep.tile([P, ROWS], U32, align_bytes=64)
+        g_scales = keep.tile([P, ROWS], U8, align_bytes=64)
+        h_grouped = keep.tile([P, FRAMES * ROWS * PACK], BF16, align_bytes=64)
+        h_codes = keep.tile([P, FRAMES, ROWS], U32, align_bytes=64)
+        h_scales = keep.tile([P, FRAMES, ROWS], U8, align_bytes=64)
+
+        g_words = g_rows[:].bitcast(F32).rearrange("p (b q u) -> p b u q", b=ROW_TILES, u=2)
+        g_t_ps = psum_acc.tile([P, ROW_TILES, 2, P], F32, name="g_t_ps", tag="acc")
+        for b in range(ROW_TILES):
+            for u in range(2):
+                nc.tensor.transpose(g_t_ps[:, b, u, :], g_words[:, b, u, :], ident_f32[:])
+        nc.vector.tensor_copy(
+            out=g_grouped[:].bitcast(F32).rearrange("p (b c u) -> p b c u", b=ROW_TILES, u=2),
+            in_=g_t_ps[:].rearrange("p b u c -> p b c u"),
+        )
+
+        h_words = h_rows[:].bitcast(F32).rearrange("p (i q u) -> p i u q", i=SLICES, u=2)
+        h_grouped_words = h_grouped[:].bitcast(F32).rearrange("p (t c u) -> p t c u", t=FRAMES, u=2)
+        for pair in range(SLICES // 2):
+            h_t_ps = psum_acc.tile([P, 2, 2, P], F32, name="h_t_ps", tag="acc")
+            for s in range(2):
+                for u in range(2):
+                    nc.tensor.transpose(h_t_ps[:, s, u, :], h_words[:, 2 * pair + s, u, :], perm_f32[:])
+            for s in range(2):
+                first_col = (2 * pair + s) * COLS_PER_SLICE
+                dst = h_grouped_words[:, :, first_col : first_col + COLS_PER_SLICE, :]
+                src = h_t_ps[:, s].rearrange("p u (t c) -> p t c u", t=FRAMES)
+                if pair % 2 == 0:
+                    nc.scalar.copy(out=dst, in_=src)
+                else:
+                    nc.vector.tensor_copy(out=dst, in_=src)
+
+        nc.vector.quantize_mx(out=g_codes[:].bitcast(FP8X4), scales=g_scales[:], in_=g_grouped[:])
+        nc.vector.quantize_mx(
+            out=h_codes[:].rearrange("p t c -> p (t c)").bitcast(FP8X4),
+            scales=h_scales[:].rearrange("p t c -> p (t c)"),
+            in_=h_grouped[:],
+        )
+
+        f_gates = keep.tile([P, FRAMES, FEAT_TILES, ROWS], F32)
+        groupeds = []
+        quantised = []
+        gates = []
+        sums = []
+        c_t_tiles = []
+
+        def regroup(step, vector_cols):
+            grouped = grouped_pool.tile([P, 2, FEATS, PACK], BF16, name="grouped", align_bytes=64)
+            split = vector_cols // RUN
+            for m in range(2):
+                src = raws[step][:, m].rearrange("p j (c i) -> p c j i", i=RUN)
+                dst = grouped[:, m].rearrange("p (c i) j -> p c j i", i=RUN)
+                nc.vector.tensor_copy(out=dst[:, :split], in_=src[:, :split])
+                nc.scalar.copy(out=dst[:, split:], in_=src[:, split:])
+            groupeds.append(grouped)
+
+        def quantise(step):
+            codes = code_pool.tile([P, 2, FEATS], U32, name="codes", align_bytes=64)
+            scales = code_pool.tile([P, 2, FEATS], U8, name="scales", align_bytes=64)
+            for m in range(2):
+                nc.vector.quantize_mx(
+                    out=codes[:, m, :].bitcast(FP8X4),
+                    scales=scales[:, m, :],
+                    in_=groupeds[step][:, m].rearrange("p n j -> p (n j)"),
+                )
+            quantised.append((codes, scales))
+
+        def multiply_and_gate(step):
+            gate, frame = divmod(step, FRAMES)
+            codes, scales = quantised[step]
+            if gate == 0:
+                dest = f_gates[:, frame]
+            else:
+                gate_tile = gate_pool.tile([P, FEAT_TILES, ROWS], F32, name="gate_tile")
+                dest = gate_tile[:]
+            gates.append(dest)
+            for pair in range(FEAT_TILES // 2):
+                acc = psum_acc.tile([P, 2, ROWS], F32, name="acc", tag="acc")
+                for s in range(2):
+                    cols = slice((2 * pair + s) * P, (2 * pair + s + 1) * P)
+                    nc.tensor.matmul_mx(
+                        out=acc[:, s, :],
+                        lhsT=codes[:, 0, cols].bitcast(FP8X4),
+                        lhsT_scale=scales[:, 0, cols],
+                        rhs=h_codes[:, frame, :].bitcast(FP8X4),
+                        rhs_scale=h_scales[:, frame, :],
+                        start=True,
+                        stop=False,
+                    )
+                    nc.tensor.matmul_mx(
+                        out=acc[:, s, :],
+                        lhsT=codes[:, 1, cols].bitcast(FP8X4),
+                        lhsT_scale=scales[:, 1, cols],
+                        rhs=g_codes[:].bitcast(FP8X4),
+                        rhs_scale=g_scales[:],
+                        start=False,
+                        stop=True,
+                    )
+                for s in range(2):
+                    column = step * FEAT_TILES + 2 * pair + s
+                    nc.scalar.activation(
+                        out=dest[:, 2 * pair + s, :],
+                        in_=acc[:, s, :],
+                        func=ACT.Sigmoid,
+                        bias=bias_cols[:, column : column + 1],
+                        scale=1.0,
+                    )
+
+        def new_sums():
+            sums.append(
+                [psum_sum.tile([P, FEATS], F32, name="sum%d" % b, tag="sum%d" % b) for b in range(ROW_TILES)]
+            )
+
+        def add_transposed_gate(step):
+            gate, frame = divmod(step, FRAMES)
+            if frame == 0:
+                new_sums()
+            for b in range(ROW_TILES):
+                for c in range(FEAT_TILES):
+                    nc.tensor.matmul(
+                        out=sums[gate][b][:, c * P : (c + 1) * P],
+                        lhsT=gates[step][:, c, b * P : (b + 1) * P],
+                        rhs=ident_f32[:],
+                        is_transpose=True,
+                        start=(frame == 0 and c == 0),
+                        stop=(frame == FRAMES - 1 and c == FEAT_TILES - 1),
+                    )
+
+        def transpose_cell_states(c):
+            c_t_ps = psum_tr.tile([P, SLICES, P], BF16, name="c_t_ps", tag="tr")
+            for i in range(SLICES):
+                nc.tensor.transpose(c_t_ps[:, i, :], c_rows[:, i, c * P : (c + 1) * P], perm_bf16[:])
+            c_t_tiles.append(c_t_ps)
+
+        def forget_products(c):
+            prod = prod_pool.tile([P, FRAMES, ROWS], F32, name="prod")
+            nc.vector.tensor_tensor(
+                out=prod[:].rearrange("p t (i c) -> p t i c", i=SLICES),
+                in0=f_gates[:, :, c, :].rearrange("p t (i c) -> p t i c", i=SLICES),
+                in1=c_t_tiles[c][:].rearrange("p i (t c) -> p t i c", t=FRAMES),
+                op=ALU.mult,
+            )
+            return prod
+
+        def add_transposed_products(c, prod):
+            for b in range(ROW_TILES):
+                for frame in range(FRAMES):
+                    nc.tensor.matmul(
+                        out=sums[0][b][:, c * P : (c + 1) * P],
+                        lhsT=prod[:, frame, b * P : (b + 1) * P],
+                        rhs=ident_f32[:],
+                        is_transpose=True,
+                        start=(frame == 0),
+                        stop=(frame == FRAMES - 1),
+                    )
+
+        kept = keep.tile([P, ROW_TILES, FEATS], F32)
+        c_out = keep.tile([P, ROW_TILES, FEATS], F32)
+        tanh_c = keep.tile([P, ROW_TILES, FEATS], F32)
+        g_out = keep.tile([P, ROW_TILES, FEATS], F32)
+        out_g = out_0.rearrange("r n f -> (r n) f").rearrange("(b p) f -> p b f", p=P)
+        out_c = out_1.rearrange("r n f -> (r n) f").rearrange("(b p) f -> p b f", p=P)
+
+        for it in range(STEPS + 2):
+            has_product = FIRST_PRODUCT <= it < FIRST_PRODUCT + FEAT_TILES
+            if 1 <= it <= STEPS:
+                quantise(it - 1)
+            if has_product:
+                prod = forget_products(it - FIRST_PRODUCT)
+            if it == COMBINE:
+                for b in range(ROW_TILES):
+                    nc.vector.scalar_tensor_tensor(
+                        out=kept[:, b, :], in0=sums[1][b][:], scalar=1.0 / FRAMES, in1=cg_rows[:, b, :],
+                        op0=ALU.mult, op1=ALU.mult,
+                    )
+                for b in range(ROW_TILES):
+                    nc.vector.scalar_tensor_tensor(
+                        out=c_out[:, b, :], in0=sums[0][b][:], scalar=1.0 / FRAMES, in1=kept[:, b, :],
+                        op0=ALU.mult, op1=ALU.add,
+                    )
+                nc.sync.dma_start(out=out_c, in_=c_out[:])
+            if it < STEPS:
+                regroup(it, VECTOR_COLS_BUSY if (has_product or it == COMBINE) else VECTOR_COLS_PLAIN)
+                if it + RAW_BUFS < STEPS:
+                    load_weights(it + RAW_BUFS)
+            if it == COMBINE:
+                nc.scalar.activation(out=tanh_c[:], in_=c_out[:], func=ACT.Tanh)
+            if 1 <= it <= STEPS:
+                multiply_and_gate(it - 1)
+            if it == FIRST_PRODUCT:
+                new_sums()
+            if has_product:
+                add_transposed_products(it - FIRST_PRODUCT, prod)
+            if FIRST_PRODUCT - 1 <= it < FIRST_PRODUCT - 1 + FEAT_TILES:
+                transpose_cell_states(it - FIRST_PRODUCT + 1)
+            if it - 2 >= FRAMES:
+                add_transposed_gate(it - 2)
+
+        for b in range(ROW_TILES):
+            nc.vector.scalar_tensor_tensor(
+                out=g_out[:, b, :], in0=sums[2][b][:], scalar=1.0 / FRAMES, in1=tanh_c[:, b, :],
+                op0=ALU.mult, op1=ALU.mult,
+            )
+            nc.sync.dma_start(out=out_g[:, b, :], in_=g_out[:, b, :])

@@ -42,8 +42,8 @@ def tile_st_hmr_pb_kernel(tc, h_new, c_new, g_t, c_g_t, Wg_t, Zg_t, bg_t, out_0,
         gate_pool = ctx.enter_context(tc.tile_pool(name="gate", bufs=3))
         prod_pool = ctx.enter_context(tc.tile_pool(name="prod", bufs=2))
         psum_sum = ctx.enter_context(tc.psum_pool(name="psum_sum", bufs=2))
-        psum_acc = ctx.enter_context(tc.psum_pool(name="psum_acc", bufs=3))
-        psum_tr = ctx.enter_context(tc.psum_pool(name="psum_tr", bufs=1))
+        psum_acc = ctx.enter_context(tc.psum_pool(name="psum_acc", bufs=4))
+        ctx.enter_context(tc.manual_schedule())
 
         bias_rows = keep.tile([P, P], BF16)
         nc.vector.memset(bias_rows[:], 0.0)
@@ -106,11 +106,6 @@ def tile_st_hmr_pb_kernel(tc, h_new, c_new, g_t, c_g_t, Wg_t, Zg_t, bg_t, out_0,
             out=perm_bf16[:].rearrange("p (t a n) -> p t a n", t=FRAMES, a=SEQS_PER_SLICE), in_=by_frame
         )
 
-        bias_ps = psum_tr.tile([P, P], BF16, name="bias_ps", tag="tr")
-        nc.tensor.transpose(bias_ps[:], bias_rows[:], ident_bf16[:])
-        bias_cols = keep.tile([P, STEPS * FEAT_TILES], F32)
-        nc.vector.tensor_copy(out=bias_cols[:], in_=bias_ps[:, 0 : STEPS * FEAT_TILES])
-
         g_grouped = keep.tile([P, ROWS * PACK], BF16, align_bytes=64)
         g_codes = keep.tile([P, ROWS], U32, align_bytes=64)
         g_scales = keep.tile([P, ROWS], U8, align_bytes=64)
@@ -144,6 +139,11 @@ def tile_st_hmr_pb_kernel(tc, h_new, c_new, g_t, c_g_t, Wg_t, Zg_t, bg_t, out_0,
                 else:
                     nc.vector.tensor_copy(out=dst, in_=src)
 
+        bias_ps = psum_acc.tile([P, P], BF16, name="bias_ps", tag="acc")
+        nc.tensor.transpose(bias_ps[:], bias_rows[:], ident_bf16[:])
+        bias_cols = keep.tile([P, STEPS * FEAT_TILES], F32)
+        nc.vector.tensor_copy(out=bias_cols[:], in_=bias_ps[:, 0 : STEPS * FEAT_TILES])
+
         nc.vector.quantize_mx(out=g_codes[:].bitcast(FP8X4), scales=g_scales[:], in_=g_grouped[:])
         nc.vector.quantize_mx(
             out=h_codes[:].rearrange("p t c -> p (t c)").bitcast(FP8X4),
@@ -171,12 +171,14 @@ def tile_st_hmr_pb_kernel(tc, h_new, c_new, g_t, c_g_t, Wg_t, Zg_t, bg_t, out_0,
         def quantise(step):
             codes = code_pool.tile([P, 2, FEATS], U32, name="codes", align_bytes=64)
             scales = code_pool.tile([P, 2, FEATS], U8, name="scales", align_bytes=64)
-            for m in range(2):
-                nc.vector.quantize_mx(
-                    out=codes[:, m, :].bitcast(FP8X4),
-                    scales=scales[:, m, :],
-                    in_=groupeds[step][:, m].rearrange("p n j -> p (n j)"),
-                )
+            for half in range(2):
+                cols = slice(half * FEATS // 2, (half + 1) * FEATS // 2)
+                for m in range(2):
+                    nc.vector.quantize_mx(
+                        out=codes[:, m, cols].bitcast(FP8X4),
+                        scales=scales[:, m, cols],
+                        in_=groupeds[step][:, m, cols, :].rearrange("p n j -> p (n j)"),
+                    )
             quantised.append((codes, scales))
 
         def multiply_and_gate(step):
@@ -229,8 +231,8 @@ def tile_st_hmr_pb_kernel(tc, h_new, c_new, g_t, c_g_t, Wg_t, Zg_t, bg_t, out_0,
             gate, frame = divmod(step, FRAMES)
             if frame == 0:
                 new_sums()
-            for b in range(ROW_TILES):
-                for c in range(FEAT_TILES):
+            for c in range(FEAT_TILES):
+                for b in range(ROW_TILES):
                     nc.tensor.matmul(
                         out=sums[gate][b][:, c * P : (c + 1) * P],
                         lhsT=gates[step][:, c, b * P : (b + 1) * P],
@@ -241,7 +243,7 @@ def tile_st_hmr_pb_kernel(tc, h_new, c_new, g_t, c_g_t, Wg_t, Zg_t, bg_t, out_0,
                     )
 
         def transpose_cell_states(c):
-            c_t_ps = psum_tr.tile([P, SLICES, P], BF16, name="c_t_ps", tag="tr")
+            c_t_ps = psum_acc.tile([P, SLICES, P], BF16, name="c_t_ps", tag="acc")
             for i in range(SLICES):
                 nc.tensor.transpose(c_t_ps[:, i, :], c_rows[:, i, c * P : (c + 1) * P], perm_bf16[:])
             c_t_tiles.append(c_t_ps)

@@ -24,8 +24,8 @@ COLS_PER_SLICE = SEQS_PER_SLICE * BONES
 STEPS = GATES * FRAMES
 RUN = 4
 RAW_BUFS = 10
-VECTOR_COLS_PLAIN = 352
-VECTOR_COLS_BUSY = 272
+VECTOR_COLS_PLAIN = 336
+VECTOR_COLS_BUSY = 256
 FIRST_PRODUCT = FRAMES + 1
 COMBINE = 2 * FRAMES + 2
 
@@ -45,52 +45,16 @@ def tile_st_hmr_pb_kernel(tc, h_new, c_new, g_t, c_g_t, Wg_t, Zg_t, bg_t, out_0,
         psum_acc = ctx.enter_context(tc.psum_pool(name="psum_acc", bufs=4))
         ctx.enter_context(tc.manual_schedule())
 
+        warm = keep.tile([P, 1], F32)
+        nc.vector.memset(warm[:], 0.0)
+        nc.scalar.activation(out=warm[:], in_=warm[:], func=ACT.Sigmoid)
+
         bias_rows = keep.tile([P, P], BF16)
         nc.vector.memset(bias_rows[:], 0.0)
         nc.scalar.dma_start(
             out=bias_rows[0 : STEPS * FEAT_TILES, :],
             in_=bg_t.rearrange("g t o (c f) -> (g t o c) f", f=P),
         )
-
-        g_rows = keep.tile([P, ROW_TILES * FEATS], BF16)
-        nc.sync.dma_start(
-            out=g_rows[:].rearrange("p (b k) -> p b k", b=ROW_TILES),
-            in_=g_t.rearrange("r n k -> (r n) k").rearrange("(b p) k -> p b k", p=P),
-        )
-        h_rows = keep.tile([P, SLICES * FEATS], BF16)
-        h_rows_view = h_rows[:].rearrange("p (i k) -> p i k", i=SLICES)
-        h_dram = h_new.rearrange("r t n k -> (r t n) k").rearrange("(i p) k -> p i k", p=P)
-        for part in range(2):
-            some = slice(part * SLICES // 2, (part + 1) * SLICES // 2)
-            nc.sync.dma_start(out=h_rows_view[:, some, :], in_=h_dram[:, some, :])
-
-        raws = []
-
-        def load_weights(step):
-            gate, frame = divmod(step, FRAMES)
-            raw = raw_pool.tile([P, 2, PACK, FEATS], BF16, name="raw")
-            nc.sync.dma_start(out=raw[:, 0], in_=Wg_t[gate, frame].rearrange("(p j) n -> p j n", j=PACK))
-            nc.sync.dma_start(out=raw[:, 1], in_=Zg_t[gate, frame].rearrange("(p j) n -> p j n", j=PACK))
-            raws.append(raw)
-
-        c_rows = keep.tile([P, SLICES, FEATS], BF16)
-        cg_rows = keep.tile([P, ROW_TILES, FEATS], BF16)
-        for step in range(RAW_BUFS):
-            load_weights(step)
-            if step == FRAMES - 1:
-                nc.sync.dma_start(
-                    out=c_rows[:],
-                    in_=c_new.rearrange("r t n k -> (r t n) k").rearrange("(i p) k -> p i k", p=P),
-                )
-            if step == 2 * FRAMES - 1:
-                nc.sync.dma_start(
-                    out=cg_rows[:],
-                    in_=c_g_t.rearrange("r n k -> (r n) k").rearrange("(b p) k -> p b k", p=P),
-                )
-
-        warm = keep.tile([P, 1], F32)
-        nc.vector.memset(warm[:], 0.0)
-        nc.scalar.activation(out=warm[:], in_=warm[:], func=ACT.Sigmoid)
 
         ident_f32 = keep.tile([P, P], F32)
         make_identity(nc, ident_f32[:])
@@ -106,50 +70,85 @@ def tile_st_hmr_pb_kernel(tc, h_new, c_new, g_t, c_g_t, Wg_t, Zg_t, bg_t, out_0,
             out=perm_bf16[:].rearrange("p (t a n) -> p t a n", t=FRAMES, a=SEQS_PER_SLICE), in_=by_frame
         )
 
+        raws = []
+
+        def load_weights(step):
+            gate, frame = divmod(step, FRAMES)
+            raw = raw_pool.tile([P, 2, PACK, FEATS], BF16, name="raw")
+            nc.sync.dma_start(out=raw[:, 0], in_=Wg_t[gate, frame].rearrange("(p j) n -> p j n", j=PACK))
+            nc.sync.dma_start(out=raw[:, 1], in_=Zg_t[gate, frame].rearrange("(p j) n -> p j n", j=PACK))
+            raws.append(raw)
+
+        g_rows = keep.tile([P, ROW_TILES * FEATS], BF16)
+        h_rows = keep.tile([P, SLICES * FEATS], BF16)
+        c_rows = keep.tile([P, SLICES, FEATS], BF16)
+        cg_rows = keep.tile([P, ROW_TILES, FEATS], BF16)
+        for step in range(RAW_BUFS):
+            load_weights(step)
+            if step == 0:
+                nc.sync.dma_start(
+                    out=g_rows[:].rearrange("p (b k) -> p b k", b=ROW_TILES),
+                    in_=g_t.rearrange("r n k -> (r n) k").rearrange("(b p) k -> p b k", p=P),
+                )
+                h_rows_view = h_rows[:].rearrange("p (i k) -> p i k", i=SLICES)
+                h_dram = h_new.rearrange("r t n k -> (r t n) k").rearrange("(i p) k -> p i k", p=P)
+                for part in range(2):
+                    some = slice(part * SLICES // 2, (part + 1) * SLICES // 2)
+                    nc.sync.dma_start(out=h_rows_view[:, some, :], in_=h_dram[:, some, :])
+            if step == FRAMES - 1:
+                nc.sync.dma_start(
+                    out=c_rows[:],
+                    in_=c_new.rearrange("r t n k -> (r t n) k").rearrange("(i p) k -> p i k", p=P),
+                )
+            if step == 2 * FRAMES - 1:
+                nc.sync.dma_start(
+                    out=cg_rows[:],
+                    in_=c_g_t.rearrange("r n k -> (r n) k").rearrange("(b p) k -> p b k", p=P),
+                )
+
         g_grouped = keep.tile([P, ROWS * PACK], BF16, align_bytes=64)
         g_codes = keep.tile([P, ROWS], U32, align_bytes=64)
         g_scales = keep.tile([P, ROWS], U8, align_bytes=64)
         h_grouped = keep.tile([P, FRAMES * ROWS * PACK], BF16, align_bytes=64)
         h_codes = keep.tile([P, FRAMES, ROWS], U32, align_bytes=64)
         h_scales = keep.tile([P, FRAMES, ROWS], U8, align_bytes=64)
-
-        g_words = g_rows[:].bitcast(F32).rearrange("p (b q u) -> p b u q", b=ROW_TILES, u=2)
-        g_t_ps = psum_acc.tile([P, ROW_TILES, 2, P], F32, name="g_t_ps", tag="acc")
-        for b in range(ROW_TILES):
-            for u in range(2):
-                nc.tensor.transpose(g_t_ps[:, b, u, :], g_words[:, b, u, :], ident_f32[:])
-        nc.vector.tensor_copy(
-            out=g_grouped[:].bitcast(F32).rearrange("p (b c u) -> p b c u", b=ROW_TILES, u=2),
-            in_=g_t_ps[:].rearrange("p b u c -> p b c u"),
-        )
-
-        h_words = h_rows[:].bitcast(F32).rearrange("p (i q u) -> p i u q", i=SLICES, u=2)
-        h_grouped_words = h_grouped[:].bitcast(F32).rearrange("p (t c u) -> p t c u", t=FRAMES, u=2)
-        for pair in range(SLICES // 2):
-            h_t_ps = psum_acc.tile([P, 2, 2, P], F32, name="h_t_ps", tag="acc")
-            for s in range(2):
-                for u in range(2):
-                    nc.tensor.transpose(h_t_ps[:, s, u, :], h_words[:, 2 * pair + s, u, :], perm_f32[:])
-            for s in range(2):
-                first_col = (2 * pair + s) * COLS_PER_SLICE
-                dst = h_grouped_words[:, :, first_col : first_col + COLS_PER_SLICE, :]
-                src = h_t_ps[:, s].rearrange("p u (t c) -> p t c u", t=FRAMES)
-                if pair % 2 == 0:
-                    nc.scalar.copy(out=dst, in_=src)
-                else:
-                    nc.vector.tensor_copy(out=dst, in_=src)
-
-        bias_ps = psum_acc.tile([P, P], BF16, name="bias_ps", tag="acc")
-        nc.tensor.transpose(bias_ps[:], bias_rows[:], ident_bf16[:])
         bias_cols = keep.tile([P, STEPS * FEAT_TILES], F32)
-        nc.vector.tensor_copy(out=bias_cols[:], in_=bias_ps[:, 0 : STEPS * FEAT_TILES])
 
-        nc.vector.quantize_mx(out=g_codes[:].bitcast(FP8X4), scales=g_scales[:], in_=g_grouped[:])
-        nc.vector.quantize_mx(
-            out=h_codes[:].rearrange("p t c -> p (t c)").bitcast(FP8X4),
-            scales=h_scales[:].rearrange("p t c -> p (t c)"),
-            in_=h_grouped[:],
-        )
+        def prepare_activations():
+            g_words = g_rows[:].bitcast(F32).rearrange("p (b q u) -> p b u q", b=ROW_TILES, u=2)
+            g_t_ps = psum_acc.tile([P, ROW_TILES, 2, P], F32, name="g_t_ps", tag="acc")
+            for b in range(ROW_TILES):
+                for u in range(2):
+                    nc.tensor.transpose(g_t_ps[:, b, u, :], g_words[:, b, u, :], ident_f32[:])
+            nc.vector.tensor_copy(
+                out=g_grouped[:].bitcast(F32).rearrange("p (b c u) -> p b c u", b=ROW_TILES, u=2),
+                in_=g_t_ps[:].rearrange("p b u c -> p b c u"),
+            )
+
+            h_words = h_rows[:].bitcast(F32).rearrange("p (i q u) -> p i u q", i=SLICES, u=2)
+            h_grouped_words = h_grouped[:].bitcast(F32).rearrange("p (t c u) -> p t c u", t=FRAMES, u=2)
+            for pair in range(SLICES // 2):
+                h_t_ps = psum_acc.tile([P, 2, 2, P], F32, name="h_t_ps", tag="acc")
+                for s in range(2):
+                    for u in range(2):
+                        nc.tensor.transpose(h_t_ps[:, s, u, :], h_words[:, 2 * pair + s, u, :], perm_f32[:])
+                for s in range(2):
+                    first_col = (2 * pair + s) * COLS_PER_SLICE
+                    nc.scalar.copy(
+                        out=h_grouped_words[:, :, first_col : first_col + COLS_PER_SLICE, :],
+                        in_=h_t_ps[:, s].rearrange("p u (t c) -> p t c u", t=FRAMES),
+                    )
+
+            bias_ps = psum_acc.tile([P, P], BF16, name="bias_ps", tag="acc")
+            nc.tensor.transpose(bias_ps[:], bias_rows[:], ident_bf16[:])
+            nc.vector.tensor_copy(out=bias_cols[:], in_=bias_ps[:, 0 : STEPS * FEAT_TILES])
+
+            nc.vector.quantize_mx(out=g_codes[:].bitcast(FP8X4), scales=g_scales[:], in_=g_grouped[:])
+            nc.vector.quantize_mx(
+                out=h_codes[:].rearrange("p t c -> p (t c)").bitcast(FP8X4),
+                scales=h_scales[:].rearrange("p t c -> p (t c)"),
+                in_=h_grouped[:],
+            )
 
         f_gates = keep.tile([P, FRAMES, FEAT_TILES, ROWS], F32)
         groupeds = []
@@ -281,6 +280,8 @@ def tile_st_hmr_pb_kernel(tc, h_new, c_new, g_t, c_g_t, Wg_t, Zg_t, bg_t, out_0,
             has_product = FIRST_PRODUCT <= it < FIRST_PRODUCT + FEAT_TILES
             if 1 <= it <= STEPS:
                 quantise(it - 1)
+            if it == 1:
+                prepare_activations()
             if has_product:
                 prod = forget_products(it - FIRST_PRODUCT)
             if it == COMBINE:

@@ -26,6 +26,12 @@ RUN = 4
 RAW_BUFS = 10
 VECTOR_COLS_PLAIN = 336
 VECTOR_COLS_BUSY = 256
+VECTOR_COLS = {}
+HALVES = 2
+S_LEAD = 1
+GROUPED_BUFS = 3
+PREP_IT = 1
+ACT_AFTER = 0
 FIRST_PRODUCT = FRAMES + 1
 COMBINE = 2 * FRAMES + 2
 
@@ -37,7 +43,7 @@ def tile_st_hmr_pb_kernel(tc, h_new, c_new, g_t, c_g_t, Wg_t, Zg_t, bg_t, out_0,
     with ExitStack() as ctx:
         keep = ctx.enter_context(tc.tile_pool(name="keep", bufs=1))
         raw_pool = ctx.enter_context(tc.tile_pool(name="raw", bufs=RAW_BUFS))
-        grouped_pool = ctx.enter_context(tc.tile_pool(name="grouped", bufs=3))
+        grouped_pool = ctx.enter_context(tc.tile_pool(name="grouped", bufs=GROUPED_BUFS))
         code_pool = ctx.enter_context(tc.tile_pool(name="code", bufs=3))
         gate_pool = ctx.enter_context(tc.tile_pool(name="gate", bufs=3))
         prod_pool = ctx.enter_context(tc.tile_pool(name="prod", bufs=2))
@@ -85,7 +91,7 @@ def tile_st_hmr_pb_kernel(tc, h_new, c_new, g_t, c_g_t, Wg_t, Zg_t, bg_t, out_0,
         cg_rows = keep.tile([P, ROW_TILES, FEATS], BF16)
         for step in range(RAW_BUFS):
             load_weights(step)
-            if step == 0:
+            if step == ACT_AFTER:
                 nc.sync.dma_start(
                     out=g_rows[:].rearrange("p (b k) -> p b k", b=ROW_TILES),
                     in_=g_t.rearrange("r n k -> (r n) k").rearrange("(b p) k -> p b k", p=P),
@@ -124,6 +130,7 @@ def tile_st_hmr_pb_kernel(tc, h_new, c_new, g_t, c_g_t, Wg_t, Zg_t, bg_t, out_0,
                 out=g_grouped[:].bitcast(F32).rearrange("p (b c u) -> p b c u", b=ROW_TILES, u=2),
                 in_=g_t_ps[:].rearrange("p b u c -> p b c u"),
             )
+            nc.vector.quantize_mx(out=g_codes[:].bitcast(FP8X4), scales=g_scales[:], in_=g_grouped[:])
 
             h_words = h_rows[:].bitcast(F32).rearrange("p (i q u) -> p i u q", i=SLICES, u=2)
             h_grouped_words = h_grouped[:].bitcast(F32).rearrange("p (t c u) -> p t c u", t=FRAMES, u=2)
@@ -139,11 +146,12 @@ def tile_st_hmr_pb_kernel(tc, h_new, c_new, g_t, c_g_t, Wg_t, Zg_t, bg_t, out_0,
                         in_=h_t_ps[:, s].rearrange("p u (t c) -> p t c u", t=FRAMES),
                     )
 
+        def turn_bias():
             bias_ps = psum_acc.tile([P, P], BF16, name="bias_ps", tag="acc")
             nc.tensor.transpose(bias_ps[:], bias_rows[:], ident_bf16[:])
             nc.vector.tensor_copy(out=bias_cols[:], in_=bias_ps[:, 0 : STEPS * FEAT_TILES])
 
-            nc.vector.quantize_mx(out=g_codes[:].bitcast(FP8X4), scales=g_scales[:], in_=g_grouped[:])
+        def quantise_hidden_states():
             nc.vector.quantize_mx(
                 out=h_codes[:].rearrange("p t c -> p (t c)").bitcast(FP8X4),
                 scales=h_scales[:].rearrange("p t c -> p (t c)"),
@@ -157,15 +165,26 @@ def tile_st_hmr_pb_kernel(tc, h_new, c_new, g_t, c_g_t, Wg_t, Zg_t, bg_t, out_0,
         sums = []
         c_t_tiles = []
 
-        def regroup(step, vector_cols):
+        def vector_cols_of(step):
+            busy = FIRST_PRODUCT <= step < FIRST_PRODUCT + FEAT_TILES or step == COMBINE
+            return VECTOR_COLS.get(step, VECTOR_COLS_BUSY if busy else VECTOR_COLS_PLAIN)
+
+        def regroup_views(step, m):
+            src = raws[step][:, m].rearrange("p j (c i) -> p c j i", i=RUN)
+            dst = groupeds[step][:, m].rearrange("p (c i) j -> p c j i", i=RUN)
+            return src, dst, vector_cols_of(step) // RUN
+
+        def regroup_on_scalar(step):
             grouped = grouped_pool.tile([P, 2, FEATS, PACK], BF16, name="grouped", align_bytes=64)
-            split = vector_cols // RUN
-            for m in range(2):
-                src = raws[step][:, m].rearrange("p j (c i) -> p c j i", i=RUN)
-                dst = grouped[:, m].rearrange("p (c i) j -> p c j i", i=RUN)
-                nc.vector.tensor_copy(out=dst[:, :split], in_=src[:, :split])
-                nc.scalar.copy(out=dst[:, split:], in_=src[:, split:])
             groupeds.append(grouped)
+            for m in range(2):
+                src, dst, split = regroup_views(step, m)
+                nc.scalar.copy(out=dst[:, split:], in_=src[:, split:])
+
+        def regroup_on_vector(step, matrices=(0, 1)):
+            for m in matrices:
+                src, dst, split = regroup_views(step, m)
+                nc.vector.tensor_copy(out=dst[:, :split], in_=src[:, :split])
 
         def quantise(step):
             codes = code_pool.tile([P, 2, FEATS], U32, name="codes", align_bytes=64)
@@ -180,16 +199,18 @@ def tile_st_hmr_pb_kernel(tc, h_new, c_new, g_t, c_g_t, Wg_t, Zg_t, bg_t, out_0,
                     )
             quantised.append((codes, scales))
 
-        def multiply_and_gate(step):
+        def multiply_and_gate(step, pairs=(0, 1)):
             gate, frame = divmod(step, FRAMES)
             codes, scales = quantised[step]
-            if gate == 0:
-                dest = f_gates[:, frame]
-            else:
-                gate_tile = gate_pool.tile([P, FEAT_TILES, ROWS], F32, name="gate_tile")
-                dest = gate_tile[:]
-            gates.append(dest)
-            for pair in range(FEAT_TILES // 2):
+            if pairs[0] == 0:
+                if gate == 0:
+                    dest = f_gates[:, frame]
+                else:
+                    gate_tile = gate_pool.tile([P, FEAT_TILES, ROWS], F32, name="gate_tile")
+                    dest = gate_tile[:]
+                gates.append(dest)
+            dest = gates[step]
+            for pair in pairs:
                 acc = psum_acc.tile([P, 2, ROWS], F32, name="acc", tag="acc")
                 for s in range(2):
                     cols = slice((2 * pair + s) * P, (2 * pair + s + 1) * P)
@@ -241,6 +262,26 @@ def tile_st_hmr_pb_kernel(tc, h_new, c_new, g_t, c_g_t, Wg_t, Zg_t, bg_t, out_0,
                         stop=(frame == FRAMES - 1 and c == FEAT_TILES - 1),
                     )
 
+        out_sums = []
+
+        def add_transposed_output_gate(step, half):
+            frame = step % FRAMES
+            if frame == 0:
+                out_sums.append(
+                    [psum_sum.tile([P, FEATS // HALVES], F32, name="osum%d" % b, tag="sum%d" % b) for b in range(ROW_TILES)]
+                )
+            per_half = FEAT_TILES // HALVES
+            for s in range(per_half):
+                for b in range(ROW_TILES):
+                    nc.tensor.matmul(
+                        out=out_sums[half][b][:, s * P : (s + 1) * P],
+                        lhsT=gates[step][:, half * per_half + s, b * P : (b + 1) * P],
+                        rhs=ident_f32[:],
+                        is_transpose=True,
+                        start=(frame == 0 and s == 0),
+                        stop=(frame == FRAMES - 1 and s == per_half - 1),
+                    )
+
         def transpose_cell_states(c):
             c_t_ps = psum_acc.tile([P, SLICES, P], BF16, name="c_t_ps", tag="acc")
             for i in range(SLICES):
@@ -272,15 +313,15 @@ def tile_st_hmr_pb_kernel(tc, h_new, c_new, g_t, c_g_t, Wg_t, Zg_t, bg_t, out_0,
         kept = keep.tile([P, ROW_TILES, FEATS], F32)
         c_out = keep.tile([P, ROW_TILES, FEATS], F32)
         tanh_c = keep.tile([P, ROW_TILES, FEATS], F32)
-        g_out = keep.tile([P, ROW_TILES, FEATS], F32)
+        g_out = [keep.tile([P, ROW_TILES, FEATS // HALVES], F32, name="g_out%d" % half) for half in range(HALVES)]
         out_g = out_0.rearrange("r n f -> (r n) f").rearrange("(b p) f -> p b f", p=P)
         out_c = out_1.rearrange("r n f -> (r n) f").rearrange("(b p) f -> p b f", p=P)
 
-        for it in range(STEPS + 2):
+        for it in range(STEPS + 1):
             has_product = FIRST_PRODUCT <= it < FIRST_PRODUCT + FEAT_TILES
             if 1 <= it <= STEPS:
                 quantise(it - 1)
-            if it == 1:
+            if it == PREP_IT:
                 prepare_activations()
             if has_product:
                 prod = forget_products(it - FIRST_PRODUCT)
@@ -296,26 +337,48 @@ def tile_st_hmr_pb_kernel(tc, h_new, c_new, g_t, c_g_t, Wg_t, Zg_t, bg_t, out_0,
                         op0=ALU.mult, op1=ALU.add,
                     )
                 nc.sync.dma_start(out=out_c, in_=c_out[:])
-            if it < STEPS:
-                regroup(it, VECTOR_COLS_BUSY if (has_product or it == COMBINE) else VECTOR_COLS_PLAIN)
-                if it + RAW_BUFS < STEPS:
-                    load_weights(it + RAW_BUFS)
+            if it < STEPS and it != 2:
+                regroup_on_scalar(it)
+            if it == 1:
+                regroup_on_vector(it, (0,))
+                quantise_hidden_states()
+                regroup_on_vector(it, (1,))
+                turn_bias()
+                regroup_on_scalar(it + 1)
+            elif it < STEPS:
+                regroup_on_vector(it)
+            if it + RAW_BUFS < STEPS:
+                load_weights(it + RAW_BUFS)
+            if it == PREP_IT:
+                for early in range(it - 1):
+                    multiply_and_gate(early)
+            if PREP_IT <= it < STEPS:
+                multiply_and_gate(it - 1)
+            if it == STEPS:
+                multiply_and_gate(it - 1)
+                for half in range(HALVES):
+                    add_transposed_output_gate(it - 2, half)
+                for half in range(HALVES):
+                    add_transposed_output_gate(it - 1, half)
             if it == COMBINE:
                 nc.scalar.activation(out=tanh_c[:], in_=c_out[:], func=ACT.Tanh)
-            if 1 <= it <= STEPS:
-                multiply_and_gate(it - 1)
             if it == FIRST_PRODUCT:
                 new_sums()
             if has_product:
                 add_transposed_products(it - FIRST_PRODUCT, prod)
             if FIRST_PRODUCT - 1 <= it < FIRST_PRODUCT - 1 + FEAT_TILES:
                 transpose_cell_states(it - FIRST_PRODUCT + 1)
-            if it - 2 >= FRAMES:
+            if FRAMES <= it - 2 < 2 * FRAMES:
                 add_transposed_gate(it - 2)
+            if 2 * FRAMES <= it - 2 and it < STEPS:
+                for half in range(HALVES):
+                    add_transposed_output_gate(it - 2, half)
 
-        for b in range(ROW_TILES):
-            nc.vector.scalar_tensor_tensor(
-                out=g_out[:, b, :], in0=sums[2][b][:], scalar=1.0 / FRAMES, in1=tanh_c[:, b, :],
-                op0=ALU.mult, op1=ALU.mult,
-            )
-            nc.sync.dma_start(out=out_g[:, b, :], in_=g_out[:, b, :])
+        for half in range(HALVES):
+            cols = slice(half * FEATS // HALVES, (half + 1) * FEATS // HALVES)
+            for b in range(ROW_TILES):
+                nc.vector.scalar_tensor_tensor(
+                    out=g_out[half][:, b, :], in0=out_sums[half][b][:], scalar=1.0 / FRAMES, in1=tanh_c[:, b, cols],
+                    op0=ALU.mult, op1=ALU.mult,
+                )
+            nc.sync.dma_start(out=out_g[:, :, cols], in_=g_out[half][:])

@@ -28,6 +28,7 @@ VECTOR_COLS_PLAIN = 336
 VECTOR_COLS_BUSY = 256
 VECTOR_COLS = {}
 HALVES = 2
+PIECES = [(b, slice(half * 256, (half + 1) * 256)) for b in range(2) for half in range(2)]
 S_LEAD = 1
 GROUPED_BUFS = 3
 PREP_IT = 1
@@ -47,8 +48,7 @@ def tile_st_hmr_pb_kernel(tc, h_new, c_new, g_t, c_g_t, Wg_t, Zg_t, bg_t, out_0,
         code_pool = ctx.enter_context(tc.tile_pool(name="code", bufs=3))
         gate_pool = ctx.enter_context(tc.tile_pool(name="gate", bufs=3))
         prod_pool = ctx.enter_context(tc.tile_pool(name="prod", bufs=2))
-        psum_sum = ctx.enter_context(tc.psum_pool(name="psum_sum", bufs=2))
-        psum_acc = ctx.enter_context(tc.psum_pool(name="psum_acc", bufs=4))
+        psum = ctx.enter_context(tc.psum_pool(name="psum", bufs=1))
         ctx.enter_context(tc.manual_schedule())
 
         warm = keep.tile([P, 1], F32)
@@ -122,7 +122,7 @@ def tile_st_hmr_pb_kernel(tc, h_new, c_new, g_t, c_g_t, Wg_t, Zg_t, bg_t, out_0,
 
         def prepare_activations():
             g_words = g_rows[:].bitcast(F32).rearrange("p (b q u) -> p b u q", b=ROW_TILES, u=2)
-            g_t_ps = psum_acc.tile([P, ROW_TILES, 2, P], F32, name="g_t_ps", tag="acc")
+            g_t_ps = psum.tile([P, ROW_TILES, 2, P], F32, name="g_t_ps", tag="f0")
             for b in range(ROW_TILES):
                 for u in range(2):
                     nc.tensor.transpose(g_t_ps[:, b, u, :], g_words[:, b, u, :], ident_f32[:])
@@ -135,7 +135,7 @@ def tile_st_hmr_pb_kernel(tc, h_new, c_new, g_t, c_g_t, Wg_t, Zg_t, bg_t, out_0,
             h_words = h_rows[:].bitcast(F32).rearrange("p (i q u) -> p i u q", i=SLICES, u=2)
             h_grouped_words = h_grouped[:].bitcast(F32).rearrange("p (t c u) -> p t c u", t=FRAMES, u=2)
             for pair in range(SLICES // 2):
-                h_t_ps = psum_acc.tile([P, 2, 2, P], F32, name="h_t_ps", tag="acc")
+                h_t_ps = psum.tile([P, 2, 2, P], F32, name="h_t_ps", tag=("f1", "g0", "g1", "o0")[pair])
                 for s in range(2):
                     for u in range(2):
                         nc.tensor.transpose(h_t_ps[:, s, u, :], h_words[:, 2 * pair + s, u, :], perm_f32[:])
@@ -147,7 +147,7 @@ def tile_st_hmr_pb_kernel(tc, h_new, c_new, g_t, c_g_t, Wg_t, Zg_t, bg_t, out_0,
                     )
 
         def turn_bias():
-            bias_ps = psum_acc.tile([P, P], BF16, name="bias_ps", tag="acc")
+            bias_ps = psum.tile([P, P], BF16, name="bias_ps", tag="o1")
             nc.tensor.transpose(bias_ps[:], bias_rows[:], ident_bf16[:])
             nc.vector.tensor_copy(out=bias_cols[:], in_=bias_ps[:, 0 : STEPS * FEAT_TILES])
 
@@ -166,7 +166,7 @@ def tile_st_hmr_pb_kernel(tc, h_new, c_new, g_t, c_g_t, Wg_t, Zg_t, bg_t, out_0,
         c_t_tiles = []
 
         def vector_cols_of(step):
-            busy = FIRST_PRODUCT <= step < FIRST_PRODUCT + FEAT_TILES or step == COMBINE
+            busy = FIRST_PRODUCT <= step < FIRST_PRODUCT + FEAT_TILES
             return VECTOR_COLS.get(step, VECTOR_COLS_BUSY if busy else VECTOR_COLS_PLAIN)
 
         def regroup_views(step, m):
@@ -211,7 +211,7 @@ def tile_st_hmr_pb_kernel(tc, h_new, c_new, g_t, c_g_t, Wg_t, Zg_t, bg_t, out_0,
                 gates.append(dest)
             dest = gates[step]
             for pair in pairs:
-                acc = psum_acc.tile([P, 2, ROWS], F32, name="acc", tag="acc")
+                acc = psum.tile([P, 2, ROWS], F32, name="acc", tag="a%d" % pair)
                 for s in range(2):
                     cols = slice((2 * pair + s) * P, (2 * pair + s + 1) * P)
                     nc.tensor.matmul_mx(
@@ -244,7 +244,7 @@ def tile_st_hmr_pb_kernel(tc, h_new, c_new, g_t, c_g_t, Wg_t, Zg_t, bg_t, out_0,
 
         def new_sums():
             sums.append(
-                [psum_sum.tile([P, FEATS], F32, name="sum%d" % b, tag="sum%d" % b) for b in range(ROW_TILES)]
+                [psum.tile([P, FEATS], F32, name="sum%d" % b, tag="%s%d" % ("fgo"[len(sums)], b)) for b in range(ROW_TILES)]
             )
 
         def add_transposed_gate(step):
@@ -262,28 +262,8 @@ def tile_st_hmr_pb_kernel(tc, h_new, c_new, g_t, c_g_t, Wg_t, Zg_t, bg_t, out_0,
                         stop=(frame == FRAMES - 1 and c == FEAT_TILES - 1),
                     )
 
-        out_sums = []
-
-        def add_transposed_output_gate(step, half):
-            frame = step % FRAMES
-            if frame == 0:
-                out_sums.append(
-                    [psum_sum.tile([P, FEATS // HALVES], F32, name="osum%d" % b, tag="sum%d" % b) for b in range(ROW_TILES)]
-                )
-            per_half = FEAT_TILES // HALVES
-            for s in range(per_half):
-                for b in range(ROW_TILES):
-                    nc.tensor.matmul(
-                        out=out_sums[half][b][:, s * P : (s + 1) * P],
-                        lhsT=gates[step][:, half * per_half + s, b * P : (b + 1) * P],
-                        rhs=ident_f32[:],
-                        is_transpose=True,
-                        start=(frame == 0 and s == 0),
-                        stop=(frame == FRAMES - 1 and s == per_half - 1),
-                    )
-
         def transpose_cell_states(c):
-            c_t_ps = psum_acc.tile([P, SLICES, P], BF16, name="c_t_ps", tag="acc")
+            c_t_ps = psum.tile([P, SLICES, P], BF16, name="c_t_ps", tag="o%d" % (c % 2))
             for i in range(SLICES):
                 nc.tensor.transpose(c_t_ps[:, i, :], c_rows[:, i, c * P : (c + 1) * P], perm_bf16[:])
             c_t_tiles.append(c_t_ps)
@@ -313,7 +293,7 @@ def tile_st_hmr_pb_kernel(tc, h_new, c_new, g_t, c_g_t, Wg_t, Zg_t, bg_t, out_0,
         kept = keep.tile([P, ROW_TILES, FEATS], F32)
         c_out = keep.tile([P, ROW_TILES, FEATS], F32)
         tanh_c = keep.tile([P, ROW_TILES, FEATS], F32)
-        g_out = [keep.tile([P, ROW_TILES, FEATS // HALVES], F32, name="g_out%d" % half) for half in range(HALVES)]
+        g_out = keep.tile([P, ROW_TILES, FEATS], F32)
         out_g = out_0.rearrange("r n f -> (r n) f").rearrange("(b p) f -> p b f", p=P)
         out_c = out_1.rearrange("r n f -> (r n) f").rearrange("(b p) f -> p b f", p=P)
 
@@ -325,18 +305,6 @@ def tile_st_hmr_pb_kernel(tc, h_new, c_new, g_t, c_g_t, Wg_t, Zg_t, bg_t, out_0,
                 prepare_activations()
             if has_product:
                 prod = forget_products(it - FIRST_PRODUCT)
-            if it == COMBINE:
-                for b in range(ROW_TILES):
-                    nc.vector.scalar_tensor_tensor(
-                        out=kept[:, b, :], in0=sums[1][b][:], scalar=1.0 / FRAMES, in1=cg_rows[:, b, :],
-                        op0=ALU.mult, op1=ALU.mult,
-                    )
-                for b in range(ROW_TILES):
-                    nc.vector.scalar_tensor_tensor(
-                        out=c_out[:, b, :], in0=sums[0][b][:], scalar=1.0 / FRAMES, in1=kept[:, b, :],
-                        op0=ALU.mult, op1=ALU.add,
-                    )
-                nc.sync.dma_start(out=out_c, in_=c_out[:])
             if it < STEPS and it != 2:
                 regroup_on_scalar(it)
             if it == 1:
@@ -356,29 +324,35 @@ def tile_st_hmr_pb_kernel(tc, h_new, c_new, g_t, c_g_t, Wg_t, Zg_t, bg_t, out_0,
                 multiply_and_gate(it - 1)
             if it == STEPS:
                 multiply_and_gate(it - 1)
-                for half in range(HALVES):
-                    add_transposed_output_gate(it - 2, half)
-                for half in range(HALVES):
-                    add_transposed_output_gate(it - 1, half)
-            if it == COMBINE:
-                nc.scalar.activation(out=tanh_c[:], in_=c_out[:], func=ACT.Tanh)
+                add_transposed_gate(it - 2)
+                add_transposed_gate(it - 1)
+            if it == STEPS:
+                for b in range(ROW_TILES):
+                    nc.vector.scalar_tensor_tensor(
+                        out=kept[:, b, :], in0=sums[1][b][:], scalar=1.0 / FRAMES, in1=cg_rows[:, b, :],
+                        op0=ALU.mult, op1=ALU.mult,
+                    )
+                for b, cols in PIECES:
+                    nc.vector.scalar_tensor_tensor(
+                        out=c_out[:, b, cols], in0=sums[0][b][:, cols], scalar=1.0 / FRAMES, in1=kept[:, b, cols],
+                        op0=ALU.mult, op1=ALU.add,
+                    )
+                    nc.scalar.activation(out=tanh_c[:, b, cols], in_=c_out[:, b, cols], func=ACT.Tanh)
+                    if cols.stop == FEATS:
+                        nc.sync.dma_start(out=out_c[:, b, :], in_=c_out[:, b, :])
             if it == FIRST_PRODUCT:
                 new_sums()
             if has_product:
                 add_transposed_products(it - FIRST_PRODUCT, prod)
             if FIRST_PRODUCT - 1 <= it < FIRST_PRODUCT - 1 + FEAT_TILES:
                 transpose_cell_states(it - FIRST_PRODUCT + 1)
-            if FRAMES <= it - 2 < 2 * FRAMES:
+            if FRAMES <= it - 2 and it < STEPS:
                 add_transposed_gate(it - 2)
-            if 2 * FRAMES <= it - 2 and it < STEPS:
-                for half in range(HALVES):
-                    add_transposed_output_gate(it - 2, half)
 
-        for half in range(HALVES):
-            cols = slice(half * FEATS // HALVES, (half + 1) * FEATS // HALVES)
-            for b in range(ROW_TILES):
-                nc.vector.scalar_tensor_tensor(
-                    out=g_out[half][:, b, :], in0=out_sums[half][b][:], scalar=1.0 / FRAMES, in1=tanh_c[:, b, cols],
-                    op0=ALU.mult, op1=ALU.mult,
-                )
-            nc.sync.dma_start(out=out_g[:, :, cols], in_=g_out[half][:])
+        for b, cols in PIECES:
+            nc.vector.scalar_tensor_tensor(
+                out=g_out[:, b, cols], in0=sums[2][b][:, cols], scalar=1.0 / FRAMES, in1=tanh_c[:, b, cols],
+                op0=ALU.mult, op1=ALU.mult,
+            )
+            if cols.stop == FEATS:
+                nc.sync.dma_start(out=out_g[:, b, :], in_=g_out[:, b, :])

@@ -115,7 +115,9 @@ def tile_st_hmr_pb_kernel(tc, h_new, c_new, g_t, c_g_t, Wg_t, Zg_t, bg_t, out_0,
         g_grouped = keep.tile([P, ROWS * PACK], BF16, align_bytes=64)
         g_codes = keep.tile([P, ROWS], U32, align_bytes=64)
         g_scales = keep.tile([P, ROWS], U8, align_bytes=64)
-        h_grouped = keep.tile([P, FRAMES * ROWS * PACK], BF16, align_bytes=64)
+        h_grouped = [
+            keep.tile([P, FRAMES * (ROWS // 2) * PACK], BF16, name="h_grouped%d" % part, align_bytes=64) for part in range(2)
+        ]
         h_codes = keep.tile([P, FRAMES, ROWS], U32, align_bytes=64)
         h_scales = keep.tile([P, FRAMES, ROWS], U8, align_bytes=64)
         bias_cols = keep.tile([P, STEPS * FEAT_TILES], F32)
@@ -133,14 +135,15 @@ def tile_st_hmr_pb_kernel(tc, h_new, c_new, g_t, c_g_t, Wg_t, Zg_t, bg_t, out_0,
             nc.vector.quantize_mx(out=g_codes[:].bitcast(FP8X4), scales=g_scales[:], in_=g_grouped[:])
 
             h_words = h_rows[:].bitcast(F32).rearrange("p (i q u) -> p i u q", i=SLICES, u=2)
-            h_grouped_words = h_grouped[:].bitcast(F32).rearrange("p (t c u) -> p t c u", t=FRAMES, u=2)
             for pair in range(SLICES // 2):
+                part = pair // (SLICES // 4)
+                h_grouped_words = h_grouped[part][:].bitcast(F32).rearrange("p (t c u) -> p t c u", t=FRAMES, u=2)
                 h_t_ps = psum.tile([P, 2, 2, P], F32, name="h_t_ps", tag=("f1", "g0", "g1", "o0")[pair])
                 for s in range(2):
                     for u in range(2):
                         nc.tensor.transpose(h_t_ps[:, s, u, :], h_words[:, 2 * pair + s, u, :], perm_f32[:])
                 for s in range(2):
-                    first_col = (2 * pair + s) * COLS_PER_SLICE
+                    first_col = (2 * pair + s) * COLS_PER_SLICE - part * ROWS // 2
                     nc.scalar.copy(
                         out=h_grouped_words[:, :, first_col : first_col + COLS_PER_SLICE, :],
                         in_=h_t_ps[:, s].rearrange("p u (t c) -> p t c u", t=FRAMES),
@@ -151,12 +154,14 @@ def tile_st_hmr_pb_kernel(tc, h_new, c_new, g_t, c_g_t, Wg_t, Zg_t, bg_t, out_0,
             nc.tensor.transpose(bias_ps[:], bias_rows[:], ident_bf16[:])
             nc.vector.tensor_copy(out=bias_cols[:], in_=bias_ps[:, 0 : STEPS * FEAT_TILES])
 
-        def quantise_hidden_states():
-            nc.vector.quantize_mx(
-                out=h_codes[:].rearrange("p t c -> p (t c)").bitcast(FP8X4),
-                scales=h_scales[:].rearrange("p t c -> p (t c)"),
-                in_=h_grouped[:],
-            )
+        def quantise_hidden_states(part):
+            cols = slice(part * ROWS // 2, (part + 1) * ROWS // 2)
+            for frame in range(FRAMES):
+                nc.vector.quantize_mx(
+                    out=h_codes[:, frame, cols].bitcast(FP8X4),
+                    scales=h_scales[:, frame, cols],
+                    in_=h_grouped[part][:].rearrange("p (t c) -> p t c", t=FRAMES)[:, frame, :],
+                )
 
         f_gates = keep.tile([P, FRAMES, FEAT_TILES, ROWS], F32)
         groupeds = []
@@ -308,8 +313,9 @@ def tile_st_hmr_pb_kernel(tc, h_new, c_new, g_t, c_g_t, Wg_t, Zg_t, bg_t, out_0,
             if it < STEPS and it != 2:
                 regroup_on_scalar(it)
             if it == 1:
+                quantise_hidden_states(0)
                 regroup_on_vector(it, (0,))
-                quantise_hidden_states()
+                quantise_hidden_states(1)
                 regroup_on_vector(it, (1,))
                 turn_bias()
                 regroup_on_scalar(it + 1)
@@ -354,5 +360,4 @@ def tile_st_hmr_pb_kernel(tc, h_new, c_new, g_t, c_g_t, Wg_t, Zg_t, bg_t, out_0,
                 out=g_out[:, b, cols], in0=sums[2][b][:, cols], scalar=1.0 / FRAMES, in1=tanh_c[:, b, cols],
                 op0=ALU.mult, op1=ALU.mult,
             )
-            if cols.stop == FEATS:
-                nc.sync.dma_start(out=out_g[:, b, :], in_=g_out[:, b, :])
+            nc.sync.dma_start(out=out_g[:, b, cols], in_=g_out[:, b, cols])

from contextlib import ExitStack

import concourse.mybir as mybir
from concourse.masks import make_identity

BF16 = mybir.dt.bfloat16
F32 = mybir.dt.float32
U32 = mybir.dt.uint32
U8 = mybir.dt.uint8
FP8X4 = mybir.dt.float8_e4m3fn_x4
ACT = mybir.ActivationFunctionType
ALU = mybir.AluOpType

P = 128
PACK = 4
SEQS, FRAMES, BONES, FEATS = 32, 4, 8, 512
GATES = 3
ROWS = SEQS * BONES
ROW_TILES = ROWS // P
FEAT_TILES = FEATS // P
SLICES = SEQS * FRAMES * BONES // P
SEQS_PER_SLICE = SEQS // SLICES
COLS_PER_SLICE = SEQS_PER_SLICE * BONES
STEPS = GATES * FRAMES
RUN = 4
RAW_BUFS = 10
VECTOR_COLS_PLAIN = 336
VECTOR_COLS_BUSY = 256
VECTOR_COLS = {}
HALVES = 2
PIECES = [(b, slice(half * 256, (half + 1) * 256)) for b in range(2) for half in range(2)]
S_LEAD = 1
GROUPED_BUFS = 3
PREP_IT = 1
ACT_AFTER = 0
FIRST_PRODUCT = FRAMES + 1
COMBINE = 2 * FRAMES + 2

FLOPS = 2 * 2 * GATES * FRAMES * ROWS * FEATS * FEATS


def tile_st_hmr_pb_kernel(tc, h_new, c_new, g_t, c_g_t, Wg_t, Zg_t, bg_t, out_0, out_1):
    nc = tc.nc
    with ExitStack() as ctx:
        keep = ctx.enter_context(tc.tile_pool(name="keep", bufs=1))
        raw_pool = ctx.enter_context(tc.tile_pool(name="raw", bufs=RAW_BUFS))
        grouped_pool = ctx.enter_context(tc.tile_pool(name="grouped", bufs=GROUPED_BUFS))
        code_pool = ctx.enter_context(tc.tile_pool(name="code", bufs=3))
        gate_pool = ctx.enter_context(tc.tile_pool(name="gate", bufs=3))
        prod_pool = ctx.enter_context(tc.tile_pool(name="prod", bufs=2))
        psum = ctx.enter_context(tc.psum_pool(name="psum", bufs=1))
        ctx.enter_context(tc.manual_schedule())

        warm = keep.tile([P, 1], F32)
        nc.vector.memset(warm[:], 0.0)
        nc.scalar.activation(out=warm[:], in_=warm[:], func=ACT.Sigmoid)

        bias_rows = keep.tile([P, P], BF16)
        nc.vector.memset(bias_rows[:], 0.0)
        nc.scalar.dma_start(
            out=bias_rows[0 : STEPS * FEAT_TILES, :],
            in_=bg_t.rearrange("g t o (c f) -> (g t o c) f", f=P),
        )

        ident_f32 = keep.tile([P, P], F32)
        make_identity(nc, ident_f32[:])
        ident_bf16 = keep.tile([P, P], BF16)
        nc.vector.tensor_copy(out=ident_bf16[:], in_=ident_f32[:])
        perm_f32 = keep.tile([P, P], F32)
        perm_bf16 = keep.tile([P, P], BF16)
        by_frame = ident_f32[:].rearrange("p (a t n) -> p t a n", a=SEQS_PER_SLICE, t=FRAMES)
        nc.vector.tensor_copy(
            out=perm_f32[:].rearrange("p (t a n) -> p t a n", t=FRAMES, a=SEQS_PER_SLICE), in_=by_frame
        )
        nc.vector.tensor_copy(
            out=perm_bf16[:].rearrange("p (t a n) -> p t a n", t=FRAMES, a=SEQS_PER_SLICE), in_=by_frame
        )

        raws = []

        def load_weights(step):
            gate, frame = divmod(step, FRAMES)
            raw = raw_pool.tile([P, 2, PACK, FEATS], BF16, name="raw")
            nc.sync.dma_start(out=raw[:, 0], in_=Wg_t[gate, frame].rearrange("(p j) n -> p j n", j=PACK))
            nc.sync.dma_start(out=raw[:, 1], in_=Zg_t[gate, frame].rearrange("(p j) n -> p j n", j=PACK))
            raws.append(raw)

        g_rows = keep.tile([P, ROW_TILES * FEATS], BF16)
        h_rows = keep.tile([P, SLICES * FEATS], BF16)
        c_rows = keep.tile([P, SLICES, FEATS], BF16)
        cg_rows = keep.tile([P, ROW_TILES, FEATS], BF16)
        for step in range(RAW_BUFS):
            load_weights(step)
            if step == ACT_AFTER:
                nc.sync.dma_start(
                    out=g_rows[:].rearrange("p (b k) -> p b k", b=ROW_TILES),
                    in_=g_t.rearrange("r n k -> (r n) k").rearrange("(b p) k -> p b k", p=P),
                )
                h_rows_view = h_rows[:].rearrange("p (i k) -> p i k", i=SLICES)
                h_dram = h_new.rearrange("r t n k -> (r t n) k").rearrange("(i p) k -> p i k", p=P)
                for part in range(2):
                    some = slice(part * SLICES // 2, (part + 1) * SLICES // 2)
                    nc.sync.dma_start(out=h_rows_view[:, some, :], in_=h_dram[:, some, :])
            if step == FRAMES - 1:
                nc.sync.dma_start(
                    out=c_rows[:],
                    in_=c_new.rearrange("r t n k -> (r t n) k").rearrange("(i p) k -> p i k", p=P),
                )
            if step == 2 * FRAMES - 1:
                nc.sync.dma_start(
                    out=cg_rows[:],
                    in_=c_g_t.rearrange("r n k -> (r n) k").rearrange("(b p) k -> p b k", p=P),
                )

        g_grouped = keep.tile([P, ROWS * PACK], BF16, align_bytes=64)
        g_codes = keep.tile([P, ROWS], U32, align_bytes=64)
        g_scales = keep.tile([P, ROWS], U8, align_bytes=64)
        h_grouped = [
            keep.tile([P, FRAMES * (ROWS // 2) * PACK], BF16, name="h_grouped%d" % part, align_bytes=64) for part in range(2)
        ]
        h_codes = keep.tile([P, FRAMES, ROWS], U32, align_bytes=64)
        h_scales = keep.tile([P, FRAMES, ROWS], U8, align_bytes=64)
        bias_cols = keep.tile([P, STEPS * FEAT_TILES], F32)

        def prepare_activations():
            g_words = g_rows[:].bitcast(F32).rearrange("p (b q u) -> p b u q", b=ROW_TILES, u=2)
            g_t_ps = psum.tile([P, ROW_TILES, 2, P], F32, name="g_t_ps", tag="f0")
            for b in range(ROW_TILES):
                for u in range(2):
                    nc.tensor.transpose(g_t_ps[:, b, u, :], g_words[:, b, u, :], ident_f32[:])
            nc.vector.tensor_copy(
                out=g_grouped[:].bitcast(F32).rearrange("p (b c u) -> p b c u", b=ROW_TILES, u=2),
                in_=g_t_ps[:].rearrange("p b u c -> p b c u"),
            )
            nc.vector.quantize_mx(out=g_codes[:].bitcast(FP8X4), scales=g_scales[:], in_=g_grouped[:])

            h_words = h_rows[:].bitcast(F32).rearrange("p (i q u) -> p i u q", i=SLICES, u=2)
            for pair in range(SLICES // 2):
                part = pair // (SLICES // 4)
                h_grouped_words = h_grouped[part][:].bitcast(F32).rearrange("p (t c u) -> p t c u", t=FRAMES, u=2)
                h_t_ps = psum.tile([P, 2, 2, P], F32, name="h_t_ps", tag=("f1", "g0", "g1", "o0")[pair])
                for s in range(2):
                    for u in range(2):
                        nc.tensor.transpose(h_t_ps[:, s, u, :], h_words[:, 2 * pair + s, u, :], perm_f32[:])
                for s in range(2):
                    first_col = (2 * pair + s) * COLS_PER_SLICE - part * ROWS // 2
                    nc.scalar.copy(
                        out=h_grouped_words[:, :, first_col : first_col + COLS_PER_SLICE, :],
                        in_=h_t_ps[:, s].rearrange("p u (t c) -> p t c u", t=FRAMES),
                    )

        def turn_bias():
            bias_ps = psum.tile([P, P], BF16, name="bias_ps", tag="o1")
            nc.tensor.transpose(bias_ps[:], bias_rows[:], ident_bf16[:])
            nc.vector.tensor_copy(out=bias_cols[:], in_=bias_ps[:, 0 : STEPS * FEAT_TILES])

        def quantise_hidden_states(part):
            cols = slice(part * ROWS // 2, (part + 1) * ROWS // 2)
            for frame in range(FRAMES):
                nc.vector.quantize_mx(
                    out=h_codes[:, frame, cols].bitcast(FP8X4),
                    scales=h_scales[:, frame, cols],
                    in_=h_grouped[part][:].rearrange("p (t c) -> p t c", t=FRAMES)[:, frame, :],
                )

        f_gates = keep.tile([P, FRAMES, FEAT_TILES, ROWS], F32)
        groupeds = []
        quantised = []
        gates = []
        sums = []
        c_t_tiles = []

        def vector_cols_of(step):
            busy = FIRST_PRODUCT <= step < FIRST_PRODUCT + FEAT_TILES
            return VECTOR_COLS.get(step, VECTOR_COLS_BUSY if busy else VECTOR_COLS_PLAIN)

        def regroup_views(step, m):
            src = raws[step][:, m].rearrange("p j (c i) -> p c j i", i=RUN)
            dst = groupeds[step][:, m].rearrange("p (c i) j -> p c j i", i=RUN)
            return src, dst, vector_cols_of(step) // RUN

        def regroup_on_scalar(step):
            grouped = grouped_pool.tile([P, 2, FEATS, PACK], BF16, name="grouped", align_bytes=64)
            groupeds.append(grouped)
            for m in range(2):
                src, dst, split = regroup_views(step, m)
                nc.scalar.copy(out=dst[:, split:], in_=src[:, split:])

        def regroup_on_vector(step, matrices=(0, 1)):
            for m in matrices:
                src, dst, split = regroup_views(step, m)
                nc.vector.tensor_copy(out=dst[:, :split], in_=src[:, :split])

        def quantise(step):
            codes = code_pool.tile([P, 2, FEATS], U32, name="codes", align_bytes=64)
            scales = code_pool.tile([P, 2, FEATS], U8, name="scales", align_bytes=64)
            for half in range(2):
                cols = slice(half * FEATS // 2, (half + 1) * FEATS // 2)
                for m in range(2):
                    nc.vector.quantize_mx(
                        out=codes[:, m, cols].bitcast(FP8X4),
                        scales=scales[:, m, cols],
                        in_=groupeds[step][:, m, cols, :].rearrange("p n j -> p (n j)"),
                    )
            quantised.append((codes, scales))

        def multiply_and_gate(step, pairs=(0, 1)):
            gate, frame = divmod(step, FRAMES)
            codes, scales = quantised[step]
            if pairs[0] == 0:
                if gate == 0:
                    dest = f_gates[:, frame]
                else:
                    gate_tile = gate_pool.tile([P, FEAT_TILES, ROWS], F32, name="gate_tile")
                    dest = gate_tile[:]
                gates.append(dest)
            dest = gates[step]
            for pair in pairs:
                acc = psum.tile([P, 2, ROWS], F32, name="acc", tag="a%d" % pair)
                for s in range(2):
                    cols = slice((2 * pair + s) * P, (2 * pair + s + 1) * P)
                    nc.tensor.matmul_mx(
                        out=acc[:, s, :],
                        lhsT=codes[:, 0, cols].bitcast(FP8X4),
                        lhsT_scale=scales[:, 0, cols],
                        rhs=h_codes[:, frame, :].bitcast(FP8X4),
                        rhs_scale=h_scales[:, frame, :],
                        start=True,
                        stop=False,
                    )
                    nc.tensor.matmul_mx(
                        out=acc[:, s, :],
                        lhsT=codes[:, 1, cols].bitcast(FP8X4),
                        lhsT_scale=scales[:, 1, cols],
                        rhs=g_codes[:].bitcast(FP8X4),
                        rhs_scale=g_scales[:],
                        start=False,
                        stop=True,
                    )
                for s in range(2):
                    column = step * FEAT_TILES + 2 * pair + s
                    nc.scalar.activation(
                        out=dest[:, 2 * pair + s, :],
                        in_=acc[:, s, :],
                        func=ACT.Sigmoid,
                        bias=bias_cols[:, column : column + 1],
                        scale=1.0,
                    )

        def new_sums():
            sums.append(
                [psum.tile([P, FEATS], F32, name="sum%d" % b, tag="%s%d" % ("fgo"[len(sums)], b)) for b in range(ROW_TILES)]
            )

        def add_transposed_gate(step):
            gate, frame = divmod(step, FRAMES)
            if frame == 0:
                new_sums()
            for c in range(FEAT_TILES):
                for b in range(ROW_TILES):
                    nc.tensor.matmul(
                        out=sums[gate][b][:, c * P : (c + 1) * P],
                        lhsT=gates[step][:, c, b * P : (b + 1) * P],
                        rhs=ident_f32[:],
                        is_transpose=True,
                        start=(frame == 0 and c == 0),
                        stop=(frame == FRAMES - 1 and c == FEAT_TILES - 1),
                    )

        def transpose_cell_states(c):
            c_t_ps = psum.tile([P, SLICES, P], BF16, name="c_t_ps", tag="o%d" % (c % 2))
            for i in range(SLICES):
                nc.tensor.transpose(c_t_ps[:, i, :], c_rows[:, i, c * P : (c + 1) * P], perm_bf16[:])
            c_t_tiles.append(c_t_ps)

        def forget_products(c):
            prod = prod_pool.tile([P, FRAMES, ROWS], F32, name="prod")
            nc.vector.tensor_tensor(
                out=prod[:].rearrange("p t (i c) -> p t i c", i=SLICES),
                in0=f_gates[:, :, c, :].rearrange("p t (i c) -> p t i c", i=SLICES),
                in1=c_t_tiles[c][:].rearrange("p i (t c) -> p t i c", t=FRAMES),
                op=ALU.mult,
            )
            return prod

        def add_transposed_products(c, prod):
            for b in range(ROW_TILES):
                for frame in range(FRAMES):
                    nc.tensor.matmul(
                        out=sums[0][b][:, c * P : (c + 1) * P],
                        lhsT=prod[:, frame, b * P : (b + 1) * P],
                        rhs=ident_f32[:],
                        is_transpose=True,
                        start=(frame == 0),
                        stop=(frame == FRAMES - 1),
                    )

        kept = keep.tile([P, ROW_TILES, FEATS], F32)
        c_out = keep.tile([P, ROW_TILES, FEATS], F32)
        tanh_c = keep.tile([P, ROW_TILES, FEATS], F32)
        g_out = keep.tile([P, ROW_TILES, FEATS], F32)
        out_g = out_0.rearrange("r n f -> (r n) f").rearrange("(b p) f -> p b f", p=P)
        out_c = out_1.rearrange("r n f -> (r n) f").rearrange("(b p) f -> p b f", p=P)

        for it in range(STEPS + 1):
            has_product = FIRST_PRODUCT <= it < FIRST_PRODUCT + FEAT_TILES
            if 1 <= it <= STEPS:
                quantise(it - 1)
            if it == PREP_IT:
                prepare_activations()
            if has_product:
                prod = forget_products(it - FIRST_PRODUCT)
            if it < STEPS and it != 2:
                regroup_on_scalar(it)
            if it == 1:
                quantise_hidden_states(0)
                regroup_on_vector(it, (0,))
                quantise_hidden_states(1)
                regroup_on_vector(it, (1,))
                turn_bias()
                regroup_on_scalar(it + 1)
            elif it < STEPS:
                regroup_on_vector(it)
            if it + RAW_BUFS < STEPS:
                load_weights(it + RAW_BUFS)
            if it == PREP_IT:
                for early in range(it - 1):
                    multiply_and_gate(early)
            if PREP_IT <= it < STEPS:
                multiply_and_gate(it - 1)
            if it == STEPS:
                multiply_and_gate(it - 1)
                add_transposed_gate(it - 2)
                add_transposed_gate(it - 1)
            if it == STEPS:
                for b in range(ROW_TILES):
                    nc.vector.scalar_tensor_tensor(
                        out=kept[:, b, :], in0=sums[1][b][:], scalar=1.0 / FRAMES, in1=cg_rows[:, b, :],
                        op0=ALU.mult, op1=ALU.mult,
                    )
                for b, cols in PIECES:
                    nc.vector.scalar_tensor_tensor(
                        out=c_out[:, b, cols], in0=sums[0][b][:, cols], scalar=1.0 / FRAMES, in1=kept[:, b, cols],
                        op0=ALU.mult, op1=ALU.add,
                    )
                    nc.scalar.activation(out=tanh_c[:, b, cols], in_=c_out[:, b, cols], func=ACT.Tanh)
                    if cols.stop == FEATS:
                        nc.sync.dma_start(out=out_c[:, b, :], in_=c_out[:, b, :])
            if it == FIRST_PRODUCT:
                new_sums()
            if has_product:
                add_transposed_products(it - FIRST_PRODUCT, prod)
            if FIRST_PRODUCT - 1 <= it < FIRST_PRODUCT - 1 + FEAT_TILES:
                transpose_cell_states(it - FIRST_PRODUCT + 1)
            if FRAMES <= it - 2 and it < STEPS:
                add_transposed_gate(it - 2)

        for b, cols in PIECES:
            nc.vector.scalar_tensor_tensor(
                out=g_out[:, b, cols], in0=sums[2][b][:, cols], scalar=1.0 / FRAMES, in1=tanh_c[:, b, cols],
                op0=ALU.mult, op1=ALU.mult,
            )
            nc.sync.dma_start(out=out_g[:, b, cols], in_=g_out[:, b, cols])
